import numpy as np
import ml_dtypes


def mxq(x, axis, fmt="e4m3"):
    dtype, down = {"e4m3": (ml_dtypes.float8_e4m3fn, 7), "e5m2": (ml_dtypes.float8_e5m2, 14)}[fmt]
    v = np.moveaxis(np.asarray(x, np.float32).astype(ml_dtypes.bfloat16).astype(np.float64), axis, -1)
    blocks = v.reshape(v.shape[:-1] + (-1, 32))
    amax = np.abs(blocks).max(-1, keepdims=True)
    byte = np.maximum(np.where(amax > 0, np.frexp(amax)[1] - 1 + 127, 0) - down, 1)
    scale = np.exp2(byte - 127.0)
    codes = (blocks / scale).astype(np.float32).astype(dtype).astype(np.float64)
    return np.moveaxis((codes * scale).reshape(v.shape), -1, axis)


WIDE = False


def mx_kscale(k):
    if not WIDE:
        return np.ones(k)
    levels = np.array([10, -10, 5, -5, 0])
    if k % 512:
        return np.exp2(np.random.permutation(np.resize(levels, k // 32))).repeat(32)
    a = np.empty((k // 512, 16))
    for p in range(k // 512):
        a[p, :8] = np.random.permutation(np.resize(levels, 8))
        for g in range(8):
            far = levels[np.abs(levels - a[p, g]) >= 10]
            a[p, g + 8] = far[np.random.randint(len(far))]
    return np.exp2(a.ravel()).repeat(32)


BF16 = ml_dtypes.bfloat16


def bf(x):
    return np.asarray(x, np.float32).astype(BF16)


def f64(x):
    return np.asarray(x).astype(np.float64)


B, K, N = 512, 16384, 512
NACT = 4


def setup_inputs():
    s = mx_kscale(K)
    g = np.tile(np.array([1.0, 1.0, 1.0, 0.5]), N // NACT)
    x = np.random.standard_normal((B, K)) * s
    weight = np.random.uniform(-1.0, 1.0, (N, K)) / np.sqrt(K) * g[:, None] / s[None, :]
    return {"x": bf(x), "weight": bf(weight)}


def reference(x, weight):
    y = mxq(f64(x), 1, "e4m3") @ mxq(f64(weight), 1, "e4m3").T
    rows, cols = y.shape
    y3 = y.reshape(rows, cols // NACT, NACT)
    out = np.stack(
        [y3[..., 0],
         np.cos(y3[..., 1]),
         np.sin(y3[..., 2]),
         np.tan(y3[..., 3])],
        axis=-1,
    )
    return out.reshape(rows, cols)

@@ -1,0 +1,199 @@
+import math
+from contextlib import ExitStack
+
+import concourse.mybir as mybir
+from concourse.masks import make_identity
+
+F32 = mybir.dt.float32
+BF16 = mybir.dt.bfloat16
+U32 = mybir.dt.uint32
+U8 = mybir.dt.uint8
+FP8X4 = mybir.dt.float8_e4m3fn_x4
+ALU = mybir.AluOpType
+ACT = mybir.ActivationFunctionType
+
+P = 128
+ROWS = 512
+K = 16384
+ROW_TILES = ROWS // P
+K_PASS = 4 * P
+PASSES = K // K_PASS
+CHUNK_K = 1024
+PASSES_PER_CHUNK = CHUNK_K // K_PASS
+CHUNKS = K // CHUNK_K
+STAGE_BUFS = 6
+UNIT = 4
+TAIL_PASSES = 2 * UNIT
+MAIN_PASSES = PASSES - TAIL_PASSES
+NACT = 4
+GROUPS = ROWS // NACT
+BANK = 512
+
+TWO_PI = 2.0 * math.pi
+ROUND_MAGIC = 1.5 * 2.0**23
+
+FLOPS = 2 * ROWS * ROWS * K
+
+
+def tile_mylayerfunc_k_kernel(tc, x, weight, out):
+    nc = tc.nc
+    with ExitStack() as ctx:
+        const = ctx.enter_context(tc.tile_pool(name="const", bufs=1))
+        stage = ctx.enter_context(tc.tile_pool(name="stage", bufs=STAGE_BUFS))
+        work = ctx.enter_context(tc.tile_pool(name="work", bufs=3))
+        x_mx = ctx.enter_context(tc.tile_pool(name="x_mx", bufs=4))
+        w_mx = ctx.enter_context(tc.tile_pool(name="w_mx", bufs=3))
+        w_last = ctx.enter_context(tc.tile_pool(name="w_last", bufs=TAIL_PASSES))
+        tail = ctx.enter_context(tc.tile_pool(name="tail", bufs=3))
+        flipped = ctx.enter_context(tc.psum_pool(name="flipped", bufs=4))
+        sums = ctx.enter_context(tc.psum_pool(name="sums", bufs=1))
+        ctx.enter_context(tc.manual_schedule())
+
+        dram = {
+            "x": x.rearrange("(t p) k -> p t k", p=P),
+            "w": weight.rearrange("(t p) k -> p t k", p=P),
+        }
+        mx_pool = {"x": x_mx, "w": w_mx, "w_last": w_last}
+        staged = {}
+
+        def load(c):
+            for name in ("x", "w"):
+                rows = stage.tile([P, ROW_TILES, CHUNK_K], BF16, name="rows_" + name)
+                nc.sync.dma_start(out=rows[:], in_=dram[name][:, :, c * CHUNK_K : (c + 1) * CHUNK_K])
+                staged[(name, c)] = rows
+
+        def block(name, t, g):
+            c, gi = divmod(g, PASSES_PER_CHUNK)
+            return staged[(name, c)][:, t, gi * K_PASS : (gi + 1) * K_PASS].bitcast(F32)
+
+        for c in range(STAGE_BUFS):
+            load(c)
+
+        ident = const.tile([P, P], F32, name="ident")
+        make_identity(nc, ident[:])
+
+        zero = const.tile([P, 1], F32, name="zero")
+        nc.vector.memset(zero[:], 0.0)
+        warm = const.tile([P, 1], F32, name="warm")
+        nc.scalar.activation(out=warm[:], in_=zero[:], func=ACT.Sin)
+
+        acc = [sums.tile([P, BANK], F32, name="acc%d" % t) for t in range(ROW_TILES)]
+
+        def flip(blocks):
+            banks = []
+            for half in range(2):
+                bank = flipped.tile([P, 2, 2, P], F32, name="bank")
+                for r in range(2):
+                    for u in range(2):
+                        nc.tensor.transpose(bank[:, r, u, :], blocks[2 * half + r][:, u : 2 * P : 2], ident[:])
+                banks.append(bank)
+            return banks
+
+        def regroup(banks, name, engines):
+            grouped = work.tile([P, UNIT * P * 4], BF16, name="grouped_" + name, align_bytes=64)
+            for half in range(2):
+                dst = grouped[:, half * 1024 : (half + 1) * 1024].bitcast(F32)
+                dst = dst.rearrange("p (r m u) -> p r m u", r=2, u=2)
+                src = banks[half][:].rearrange("p r u m -> p r m u")
+                if engines[half] == "vector":
+                    nc.vector.tensor_copy(out=dst, in_=src)
+                else:
+                    nc.scalar.copy(out=dst, in_=src)
+            return grouped
+
+        def quantise(grouped, name):
+            codes = mx_pool[name].tile([P, UNIT * P], U32, name="codes_" + name, align_bytes=64)
+            scales = mx_pool[name].tile([P, UNIT * P], U8, name="scales_" + name, align_bytes=64)
+            nc.vector.quantize_mx(out=codes[:].bitcast(FP8X4), scales=scales[:], in_=grouped[:])
+            return codes, scales
+
+        def empty_round(banks, last_engine):
+            first = regroup(banks[0:2], "a", ("scalar", "scalar"))
+            second = regroup(banks[2:4], "b", ("scalar", last_engine))
+            return first, second
+
+        def mx_pass(t, x_unit, j, w_unit, start, stop):
+            cols = slice(j * P, (j + 1) * P)
+            nc.tensor.matmul_mx(
+                out=acc[t][:],
+                lhsT=x_unit[0][:, cols].bitcast(FP8X4),
+                lhsT_scale=x_unit[1][:, cols],
+                rhs=w_unit[0][:].bitcast(FP8X4),
+                rhs_scale=w_unit[1][:],
+                start=start,
+                stop=stop,
+            )
+
+        x_units = {}
+        w_units = {}
+
+        def multiply_pass(g):
+            for t in range(ROW_TILES):
+                mx_pass(t, x_units[g], t, w_units[g], g == 0, False)
+
+        for g in range(MAIN_PASSES):
+            banks = flip([block("x", t, g) for t in range(ROW_TILES)])
+            banks += flip([block("w", t, g) for t in range(ROW_TILES)])
+            x_grouped, w_grouped = empty_round(banks, "vector")
+            ahead = MAIN_PASSES + 2 * (g - (MAIN_PASSES - TAIL_PASSES // 2))
+            if ahead >= MAIN_PASSES:
+                banks = flip([block("w", t, ahead) for t in range(ROW_TILES)])
+                banks += flip([block("w", t, ahead + 1) for t in range(ROW_TILES)])
+            if g > 0:
+                multiply_pass(g - 1)
+            x_units[g] = quantise(x_grouped, "x")
+            w_units[g] = quantise(w_grouped, "w")
+            if ahead >= MAIN_PASSES:
+                first, second = empty_round(banks, "vector")
+                w_units[ahead] = quantise(first, "w_last")
+                w_units[ahead + 1] = quantise(second, "w_last")
+            c, gi = divmod(g, PASSES_PER_CHUNK)
+            if gi == PASSES_PER_CHUNK - 1 and c + STAGE_BUFS < CHUNKS:
+                load(c + STAGE_BUFS)
+
+        def multiply_tile(t, units):
+            for j in range(TAIL_PASSES):
+                mx_pass(t, units[j // UNIT], j % UNIT, w_units[MAIN_PASSES + j], False, j == TAIL_PASSES - 1)
+
+        def angles(t):
+            y = acc[t][:].rearrange("p (g c) -> p c g", c=NACT)
+            turns = tail.tile([P, 5, GROUPS], F32, name="turns")
+            res = tail.tile([P, 5, GROUPS], F32, name="res")
+            nc.scalar.activation(out=turns[:, 1:5:3, :], in_=y[:, 1:4:2, :], func=ACT.Copy, bias=0.25, scale=1.0 / TWO_PI)
+            nc.scalar.activation(out=turns[:, 2:4, :], in_=y[:, 2:4, :], func=ACT.Copy, scale=1.0 / TWO_PI)
+            nc.scalar.copy(out=res[:, 0, :], in_=y[:, 0, :])
+            whole = tail.tile([P, 4, GROUPS], F32, name="whole")
+            nc.vector.tensor_scalar(
+                out=whole[:], in0=turns[:, 1:5, :], scalar1=ROUND_MAGIC, scalar2=ROUND_MAGIC, op0=ALU.add, op1=ALU.subtract
+            )
+            frac = tail.tile([P, 4, GROUPS], F32, name="frac")
+            nc.vector.tensor_tensor(out=frac[:], in0=turns[:, 1:5, :], in1=whole[:], op=ALU.subtract)
+            return frac, res
+
+        def finish(t, frac, res):
+            nc.scalar.activation(out=res[:, 4, :], in_=frac[:, 3, :], func=ACT.Sin, scale=TWO_PI)
+            nc.scalar.activation(out=res[:, 1:4, :], in_=frac[:, 0:3, :], func=ACT.Sin, scale=TWO_PI)
+            sec = tail.tile([P, GROUPS], F32, name="sec")
+            nc.vector.reciprocal(out=sec[:], in_=res[:, 4, :])
+            nc.vector.tensor_mul(res[:, 3, :], res[:, 3, :], sec[:])
+            woven = tail.tile([P, GROUPS, NACT], F32, name="woven")
+            nc.vector.tensor_copy(out=woven[:], in_=res[:, 0:4, :].rearrange("p c g -> p g c"))
+            nc.sync.dma_start(out=out[t * P : (t + 1) * P, :], in_=woven[:].rearrange("p g c -> p (g c)"))
+
+        tile_units = {}
+        halfway = {}
+        for i in range(ROW_TILES + 2):
+            if i < ROW_TILES:
+                banks = flip([block("x", i, MAIN_PASSES + j) for j in range(UNIT)])
+                banks += flip([block("x", i, MAIN_PASSES + UNIT + j) for j in range(UNIT)])
+            if i == 0:
+                multiply_pass(MAIN_PASSES - 1)
+            if 1 <= i <= ROW_TILES:
+                multiply_tile(i - 1, tile_units[i - 1])
+            if i < ROW_TILES:
+                first, second = empty_round(banks, "scalar")
+                tile_units[i] = (quantise(first, "x"), quantise(second, "x"))
+            if i >= 2:
+                finish(i - 2, halfway[i - 2][0], halfway[i - 2][1])
+            if 1 <= i <= ROW_TILES:
+                halfway[i - 1] = angles(i - 1)

@@ -21,7 +21,9 @@ PASSES = K // K_PASS
 CHUNK_K = 1024
 PASSES_PER_CHUNK = CHUNK_K // K_PASS
 CHUNKS = K // CHUNK_K
-STAGE_BUFS = 6
+STAGE_BUFS = 4
+RUN = 16
+AHEAD = 4
 UNIT = 4
 TAIL_PASSES = 2 * UNIT
 MAIN_PASSES = PASSES - TAIL_PASSES
@@ -40,6 +42,8 @@ def tile_mylayerfunc_k_kernel(tc, x, weight, out):
     with ExitStack() as ctx:
         const = ctx.enter_context(tc.tile_pool(name="const", bufs=1))
         stage = ctx.enter_context(tc.tile_pool(name="stage", bufs=STAGE_BUFS))
+        x_split = ctx.enter_context(tc.tile_pool(name="x_split", bufs=TAIL_PASSES + 3))
+        w_split = ctx.enter_context(tc.tile_pool(name="w_split", bufs=5))
         work = ctx.enter_context(tc.tile_pool(name="work", bufs=3))
         x_mx = ctx.enter_context(tc.tile_pool(name="x_mx", bufs=4))
         w_mx = ctx.enter_context(tc.tile_pool(name="w_mx", bufs=3))
@@ -54,20 +58,60 @@ def tile_mylayerfunc_k_kernel(tc, x, weight, out):
             "w": weight.rearrange("(t p) k -> p t k", p=P),
         }
         mx_pool = {"x": x_mx, "w": w_mx, "w_last": w_last}
-        staged = {}
+        split_pool = {"x": x_split, "w": w_split}
 
-        def load(c):
-            for name in ("x", "w"):
-                rows = stage.tile([P, ROW_TILES, CHUNK_K], BF16, name="rows_" + name)
+        order = []
+        for g in range(MAIN_PASSES):
+            order += [("x", g), ("w", g)]
+            ahead = MAIN_PASSES + 2 * (g - (MAIN_PASSES - TAIL_PASSES // 2))
+            if ahead >= MAIN_PASSES:
+                order += [("w", ahead), ("w", ahead + 1)]
+        order += [("x", MAIN_PASSES + j) for j in range(TAIL_PASSES)]
+        chunk_order = []
+        for name, g in order:
+            if (name, g // PASSES_PER_CHUNK) not in chunk_order:
+                chunk_order.append((name, g // PASSES_PER_CHUNK))
+
+        staged = {}
+        in_use = {"x": [], "w": []}
+        done = set()
+        split = {}
+
+        def load_what_fits():
+            while chunk_order:
+                name, c = chunk_order[0]
+                held = in_use[name]
+                if len(held) == STAGE_BUFS:
+                    if (name, held[0]) not in done:
+                        return
+                    held.pop(0)
+                held.append(c)
+                chunk_order.pop(0)
+                rows = stage.tile([P, ROW_TILES, CHUNK_K], BF16, name="rows_" + name, align_bytes=64)
                 nc.sync.dma_start(out=rows[:], in_=dram[name][:, :, c * CHUNK_K : (c + 1) * CHUNK_K])
                 staged[(name, c)] = rows
 
-        def block(name, t, g):
+        def split_next():
+            if not order:
+                return
+            name, g = order.pop(0)
             c, gi = divmod(g, PASSES_PER_CHUNK)
-            return staged[(name, c)][:, t, gi * K_PASS : (gi + 1) * K_PASS].bitcast(F32)
+            halves = split_pool[name].tile([P, ROW_TILES, K_PASS], BF16, name="halves_" + name, align_bytes=64)
+            nc.vector.tensor_copy(
+                out=halves[:].rearrange("p t (h b i) -> p t h b i", h=2, i=RUN),
+                in_=staged[(name, c)][:, :, gi * K_PASS : (gi + 1) * K_PASS].rearrange(
+                    "p t (b h i) -> p t h b i", h=2, i=RUN
+                ),
+            )
+            split[(name, g)] = halves
+            if gi == PASSES_PER_CHUNK - 1:
+                done.add((name, c))
+                load_what_fits()
 
-        for c in range(STAGE_BUFS):
-            load(c)
+        def block(name, t, g):
+            return split[(name, g)][:, t, :].bitcast(F32)
+
+        load_what_fits()
 
         ident = const.tile([P, P], F32, name="ident")
         make_identity(nc, ident[:])
@@ -85,7 +129,7 @@ def tile_mylayerfunc_k_kernel(tc, x, weight, out):
                 bank = flipped.tile([P, 2, 2, P], F32, name="bank")
                 for r in range(2):
                     for u in range(2):
-                        nc.tensor.transpose(bank[:, r, u, :], blocks[2 * half + r][:, u : 2 * P : 2], ident[:])
+                        nc.tensor.transpose(bank[:, r, u, :], blocks[2 * half + r][:, u * P : (u + 1) * P], ident[:])
                 banks.append(bank)
             return banks
 
@@ -131,25 +175,30 @@ def tile_mylayerfunc_k_kernel(tc, x, weight, out):
             for t in range(ROW_TILES):
                 mx_pass(t, x_units[g], t, w_units[g], g == 0, False)
 
+        for j in range(AHEAD):
+            split_next()
         for g in range(MAIN_PASSES):
             banks = flip([block("x", t, g) for t in range(ROW_TILES)])
             banks += flip([block("w", t, g) for t in range(ROW_TILES)])
-            x_grouped, w_grouped = empty_round(banks, "vector")
+            x_grouped, w_grouped = empty_round(banks, "scalar")
             ahead = MAIN_PASSES + 2 * (g - (MAIN_PASSES - TAIL_PASSES // 2))
             if ahead >= MAIN_PASSES:
                 banks = flip([block("w", t, ahead) for t in range(ROW_TILES)])
                 banks += flip([block("w", t, ahead + 1) for t in range(ROW_TILES)])
             if g > 0:
                 multiply_pass(g - 1)
+            split_next()
             x_units[g] = quantise(x_grouped, "x")
+            split_next()
             w_units[g] = quantise(w_grouped, "w")
             if ahead >= MAIN_PASSES:
-                first, second = empty_round(banks, "vector")
+                first, second = empty_round(banks, "scalar")
+                split_next()
                 w_units[ahead] = quantise(first, "w_last")
+                split_next()
                 w_units[ahead + 1] = quantise(second, "w_last")
-            c, gi = divmod(g, PASSES_PER_CHUNK)
-            if gi == PASSES_PER_CHUNK - 1 and c + STAGE_BUFS < CHUNKS:
-                load(c + STAGE_BUFS)
+        while order:
+            split_next()
 
         def multiply_tile(t, units):
             for j in range(TAIL_PASSES):

@@ -25,7 +25,7 @@ STAGE_BUFS = 4
 RUN = 16
 AHEAD = 4
 UNIT = 4
-TAIL_PASSES = 2 * UNIT
+TAIL_PASSES = UNIT
 MAIN_PASSES = PASSES - TAIL_PASSES
 NACT = 4
 GROUPS = ROWS // NACT
@@ -63,9 +63,8 @@ def tile_mylayerfunc_k_kernel(tc, x, weight, out):
         order = []
         for g in range(MAIN_PASSES):
             order += [("x", g), ("w", g)]
-            ahead = MAIN_PASSES + 2 * (g - (MAIN_PASSES - TAIL_PASSES // 2))
-            if ahead >= MAIN_PASSES:
-                order += [("w", ahead), ("w", ahead + 1)]
+            if g + TAIL_PASSES >= MAIN_PASSES:
+                order.append(("w", g + TAIL_PASSES))
         order += [("x", MAIN_PASSES + j) for j in range(TAIL_PASSES)]
         chunk_order = []
         for name, g in order:
@@ -181,10 +180,9 @@ def tile_mylayerfunc_k_kernel(tc, x, weight, out):
             banks = flip([block("x", t, g) for t in range(ROW_TILES)])
             banks += flip([block("w", t, g) for t in range(ROW_TILES)])
             x_grouped, w_grouped = empty_round(banks, "scalar")
-            ahead = MAIN_PASSES + 2 * (g - (MAIN_PASSES - TAIL_PASSES // 2))
+            ahead = g + TAIL_PASSES
             if ahead >= MAIN_PASSES:
                 banks = flip([block("w", t, ahead) for t in range(ROW_TILES)])
-                banks += flip([block("w", t, ahead + 1) for t in range(ROW_TILES)])
             if g > 0:
                 multiply_pass(g - 1)
             split_next()
@@ -192,17 +190,15 @@ def tile_mylayerfunc_k_kernel(tc, x, weight, out):
             split_next()
             w_units[g] = quantise(w_grouped, "w")
             if ahead >= MAIN_PASSES:
-                first, second = empty_round(banks, "scalar")
+                grouped = regroup(banks, "a", ("scalar", "scalar"))
                 split_next()
-                w_units[ahead] = quantise(first, "w_last")
-                split_next()
-                w_units[ahead + 1] = quantise(second, "w_last")
+                w_units[ahead] = quantise(grouped, "w_last")
         while order:
             split_next()
 
         def multiply_tile(t, units):
             for j in range(TAIL_PASSES):
-                mx_pass(t, units[j // UNIT], j % UNIT, w_units[MAIN_PASSES + j], False, j == TAIL_PASSES - 1)
+                mx_pass(t, units, j, w_units[MAIN_PASSES + j], False, j == TAIL_PASSES - 1)
 
         def angles(t):
             y = acc[t][:].rearrange("p (g c) -> p c g", c=NACT)
@@ -234,14 +230,12 @@ def tile_mylayerfunc_k_kernel(tc, x, weight, out):
         for i in range(ROW_TILES + 2):
             if i < ROW_TILES:
                 banks = flip([block("x", i, MAIN_PASSES + j) for j in range(UNIT)])
-                banks += flip([block("x", i, MAIN_PASSES + UNIT + j) for j in range(UNIT)])
             if i == 0:
                 multiply_pass(MAIN_PASSES - 1)
             if 1 <= i <= ROW_TILES:
                 multiply_tile(i - 1, tile_units[i - 1])
             if i < ROW_TILES:
-                first, second = empty_round(banks, "scalar")
-                tile_units[i] = (quantise(first, "x"), quantise(second, "x"))
+                tile_units[i] = quantise(regroup(banks, "a", ("scalar", "scalar")), "x")
             if i >= 2:
                 finish(i - 2, halfway[i - 2][0], halfway[i - 2][1])
             if 1 <= i <= ROW_TILES:

@@ -18,12 +18,10 @@ K = 16384
 ROW_TILES = ROWS // P
 K_PASS = 4 * P
 PASSES = K // K_PASS
-CHUNK_K = 1024
-PASSES_PER_CHUNK = CHUNK_K // K_PASS
-CHUNKS = K // CHUNK_K
+LOAD_PASSES = 2
 STAGE_BUFS = 4
 RUN = 16
-AHEAD = 4
+AHEAD = 2
 UNIT = 4
 TAIL_PASSES = UNIT
 MAIN_PASSES = PASSES - TAIL_PASSES
@@ -42,10 +40,12 @@ def tile_mylayerfunc_k_kernel(tc, x, weight, out):
     with ExitStack() as ctx:
         const = ctx.enter_context(tc.tile_pool(name="const", bufs=1))
         stage = ctx.enter_context(tc.tile_pool(name="stage", bufs=STAGE_BUFS))
-        x_split = ctx.enter_context(tc.tile_pool(name="x_split", bufs=TAIL_PASSES + 3))
-        w_split = ctx.enter_context(tc.tile_pool(name="w_split", bufs=5))
+        x_split = ctx.enter_context(tc.tile_pool(name="x_split", bufs=AHEAD + 2))
+        x_last = ctx.enter_context(tc.tile_pool(name="x_last", bufs=TAIL_PASSES))
+        w_split = ctx.enter_context(tc.tile_pool(name="w_split", bufs=AHEAD + 4))
         work = ctx.enter_context(tc.tile_pool(name="work", bufs=3))
-        x_mx = ctx.enter_context(tc.tile_pool(name="x_mx", bufs=4))
+        x_mx = ctx.enter_context(tc.tile_pool(name="x_mx", bufs=3))
+        x_tail = ctx.enter_context(tc.tile_pool(name="x_tail", bufs=ROW_TILES))
         w_mx = ctx.enter_context(tc.tile_pool(name="w_mx", bufs=3))
         w_last = ctx.enter_context(tc.tile_pool(name="w_last", bufs=TAIL_PASSES))
         tail = ctx.enter_context(tc.tile_pool(name="tail", bufs=3))
@@ -57,19 +57,28 @@ def tile_mylayerfunc_k_kernel(tc, x, weight, out):
             "x": x.rearrange("(t p) k -> p t k", p=P),
             "w": weight.rearrange("(t p) k -> p t k", p=P),
         }
-        mx_pool = {"x": x_mx, "w": w_mx, "w_last": w_last}
+        mx_pool = {"x": x_mx, "w": w_mx, "w_last": w_last, "x_tail": x_tail}
         split_pool = {"x": x_split, "w": w_split}
 
-        order = []
-        for g in range(MAIN_PASSES):
-            order += [("x", g), ("w", g)]
-            if g + TAIL_PASSES >= MAIN_PASSES:
-                order.append(("w", g + TAIL_PASSES))
-        order += [("x", MAIN_PASSES + j) for j in range(TAIL_PASSES)]
+        needs = [[("x", g), ("w", g)] for g in range(MAIN_PASSES)]
+        extra_w = {}
+        extra_x = {}
+        for j in range(TAIL_PASSES):
+            g = MAIN_PASSES - 3 * TAIL_PASSES + 2 * j
+            extra_w[g] = MAIN_PASSES + j
+            needs[g].append(("w", MAIN_PASSES + j))
+            needs[g + 1].append(("x", MAIN_PASSES + j))
+        for t in range(ROW_TILES):
+            extra_x[MAIN_PASSES - ROW_TILES + t] = t
+
+        chunk_of = {}
         chunk_order = []
-        for name, g in order:
-            if (name, g // PASSES_PER_CHUNK) not in chunk_order:
-                chunk_order.append((name, g // PASSES_PER_CHUNK))
+        for name, g in [item for items in needs for item in items]:
+            if (name, g) not in chunk_of:
+                first, passes = (g, 1) if g < LOAD_PASSES else (g - g % LOAD_PASSES, LOAD_PASSES)
+                chunk_order.append((name, first, passes))
+                for j in range(passes):
+                    chunk_of[(name, first + j)] = first
 
         staged = {}
         in_use = {"x": [], "w": []}
@@ -78,33 +87,35 @@ def tile_mylayerfunc_k_kernel(tc, x, weight, out):
 
         def load_what_fits():
             while chunk_order:
-                name, c = chunk_order[0]
+                name, first, passes = chunk_order[0]
                 held = in_use[name]
                 if len(held) == STAGE_BUFS:
                     if (name, held[0]) not in done:
                         return
                     held.pop(0)
-                held.append(c)
+                held.append(first)
                 chunk_order.pop(0)
-                rows = stage.tile([P, ROW_TILES, CHUNK_K], BF16, name="rows_" + name, align_bytes=64)
-                nc.sync.dma_start(out=rows[:], in_=dram[name][:, :, c * CHUNK_K : (c + 1) * CHUNK_K])
-                staged[(name, c)] = rows
+                rows = stage.tile([P, ROW_TILES, LOAD_PASSES * K_PASS], BF16, name="rows_" + name, align_bytes=64)
+                nc.sync.dma_start(
+                    out=rows[:, :, 0 : passes * K_PASS],
+                    in_=dram[name][:, :, first * K_PASS : (first + passes) * K_PASS],
+                )
+                staged[(name, first)] = rows
 
-        def split_next():
-            if not order:
-                return
-            name, g = order.pop(0)
-            c, gi = divmod(g, PASSES_PER_CHUNK)
-            halves = split_pool[name].tile([P, ROW_TILES, K_PASS], BF16, name="halves_" + name, align_bytes=64)
+        def split_pass(name, g):
+            first = chunk_of[(name, g)]
+            gi = g - first
+            pool = x_last if name == "x" and g >= MAIN_PASSES else split_pool[name]
+            halves = pool.tile([P, ROW_TILES, K_PASS], BF16, name="halves_" + name, align_bytes=64)
             nc.vector.tensor_copy(
                 out=halves[:].rearrange("p t (h b i) -> p t h b i", h=2, i=RUN),
-                in_=staged[(name, c)][:, :, gi * K_PASS : (gi + 1) * K_PASS].rearrange(
+                in_=staged[(name, first)][:, :, gi * K_PASS : (gi + 1) * K_PASS].rearrange(
                     "p t (b h i) -> p t h b i", h=2, i=RUN
                 ),
             )
             split[(name, g)] = halves
-            if gi == PASSES_PER_CHUNK - 1:
-                done.add((name, c))
+            if chunk_of.get((name, g + 1)) != first:
+                done.add((name, first))
                 load_what_fits()
 
         def block(name, t, g):
@@ -169,34 +180,39 @@ def tile_mylayerfunc_k_kernel(tc, x, weight, out):
 
         x_units = {}
         w_units = {}
+        tile_units = {}
 
         def multiply_pass(g):
             for t in range(ROW_TILES):
                 mx_pass(t, x_units[g], t, w_units[g], g == 0, False)
 
-        for j in range(AHEAD):
-            split_next()
+        for items in needs[:AHEAD]:
+            for name, g in items:
+                split_pass(name, g)
         for g in range(MAIN_PASSES):
+            todo = needs[g + AHEAD] if g + AHEAD < MAIN_PASSES else []
             banks = flip([block("x", t, g) for t in range(ROW_TILES)])
             banks += flip([block("w", t, g) for t in range(ROW_TILES)])
             x_grouped, w_grouped = empty_round(banks, "scalar")
-            ahead = g + TAIL_PASSES
-            if ahead >= MAIN_PASSES:
-                banks = flip([block("w", t, ahead) for t in range(ROW_TILES)])
+            if g in extra_w:
+                banks = flip([block("w", t, extra_w[g]) for t in range(ROW_TILES)])
+            if g in extra_x:
+                banks = flip([block("x", extra_x[g], MAIN_PASSES + j) for j in range(TAIL_PASSES)])
             if g > 0:
                 multiply_pass(g - 1)
-            split_next()
             x_units[g] = quantise(x_grouped, "x")
-            split_next()
+            for name, later in todo[0:1]:
+                split_pass(name, later)
             w_units[g] = quantise(w_grouped, "w")
-            if ahead >= MAIN_PASSES:
-                grouped = regroup(banks, "a", ("scalar", "scalar"))
-                split_next()
-                w_units[ahead] = quantise(grouped, "w_last")
-        while order:
-            split_next()
+            for name, later in todo[1:]:
+                split_pass(name, later)
+            if g in extra_w:
+                w_units[extra_w[g]] = quantise(regroup(banks, "a", ("scalar", "scalar")), "w_last")
+            if g in extra_x:
+                tile_units[extra_x[g]] = quantise(regroup(banks, "a", ("scalar", "scalar")), "x_tail")
 
         def multiply_tile(t, units):
+            mx_pass(t, x_units[MAIN_PASSES - 1], t, w_units[MAIN_PASSES - 1], False, False)
             for j in range(TAIL_PASSES):
                 mx_pass(t, units, j, w_units[MAIN_PASSES + j], False, j == TAIL_PASSES - 1)
 
@@ -215,28 +231,31 @@ def tile_mylayerfunc_k_kernel(tc, x, weight, out):
             nc.vector.tensor_tensor(out=frac[:], in0=turns[:, 1:5, :], in1=whole[:], op=ALU.subtract)
             return frac, res
 
-        def finish(t, frac, res):
+        def sines(frac, res):
             nc.scalar.activation(out=res[:, 4, :], in_=frac[:, 3, :], func=ACT.Sin, scale=TWO_PI)
             nc.scalar.activation(out=res[:, 1:4, :], in_=frac[:, 0:3, :], func=ACT.Sin, scale=TWO_PI)
+
+        def tangent(res):
             sec = tail.tile([P, GROUPS], F32, name="sec")
             nc.vector.reciprocal(out=sec[:], in_=res[:, 4, :])
             nc.vector.tensor_mul(res[:, 3, :], res[:, 3, :], sec[:])
+
+        def store(t, res):
             woven = tail.tile([P, GROUPS, NACT], F32, name="woven")
-            nc.vector.tensor_copy(out=woven[:], in_=res[:, 0:4, :].rearrange("p c g -> p g c"))
+            by_column = res[:, 0:4, :].rearrange("p c g -> p g c")
+            if t == ROW_TILES - 1:
+                nc.vector.tensor_copy(out=woven[:], in_=by_column)
+            else:
+                nc.scalar.copy(out=woven[:], in_=by_column)
             nc.sync.dma_start(out=out[t * P : (t + 1) * P, :], in_=woven[:].rearrange("p g c -> p (g c)"))
 
-        tile_units = {}
         halfway = {}
-        for i in range(ROW_TILES + 2):
-            if i < ROW_TILES:
-                banks = flip([block("x", i, MAIN_PASSES + j) for j in range(UNIT)])
-            if i == 0:
-                multiply_pass(MAIN_PASSES - 1)
-            if 1 <= i <= ROW_TILES:
-                multiply_tile(i - 1, tile_units[i - 1])
-            if i < ROW_TILES:
-                tile_units[i] = quantise(regroup(banks, "a", ("scalar", "scalar")), "x")
-            if i >= 2:
-                finish(i - 2, halfway[i - 2][0], halfway[i - 2][1])
-            if 1 <= i <= ROW_TILES:
-                halfway[i - 1] = angles(i - 1)
+        for t in range(ROW_TILES + 2):
+            if t < ROW_TILES:
+                multiply_tile(t, tile_units[t])
+                halfway[t] = angles(t)
+            if 0 <= t - 1 < ROW_TILES:
+                sines(*halfway[t - 1])
+                tangent(halfway[t - 1][1])
+            if t - 2 >= 0:
+                store(t - 2, halfway[t - 2][1])

@@ -21,6 +21,7 @@ PASSES = K // K_PASS
 LOAD_PASSES = 2
 STAGE_BUFS = 4
 RUN = 16
+LAG = 2
 AHEAD = 2
 UNIT = 4
 TAIL_PASSES = UNIT
@@ -44,9 +45,9 @@ def tile_mylayerfunc_k_kernel(tc, x, weight, out):
         x_last = ctx.enter_context(tc.tile_pool(name="x_last", bufs=TAIL_PASSES))
         w_split = ctx.enter_context(tc.tile_pool(name="w_split", bufs=AHEAD + 4))
         work = ctx.enter_context(tc.tile_pool(name="work", bufs=3))
-        x_mx = ctx.enter_context(tc.tile_pool(name="x_mx", bufs=3))
+        x_mx = ctx.enter_context(tc.tile_pool(name="x_mx", bufs=LAG + 2))
         x_tail = ctx.enter_context(tc.tile_pool(name="x_tail", bufs=ROW_TILES))
-        w_mx = ctx.enter_context(tc.tile_pool(name="w_mx", bufs=3))
+        w_mx = ctx.enter_context(tc.tile_pool(name="w_mx", bufs=LAG + 2))
         w_last = ctx.enter_context(tc.tile_pool(name="w_last", bufs=TAIL_PASSES))
         tail = ctx.enter_context(tc.tile_pool(name="tail", bufs=3))
         flipped = ctx.enter_context(tc.psum_pool(name="flipped", bufs=4))
@@ -198,8 +199,8 @@ def tile_mylayerfunc_k_kernel(tc, x, weight, out):
                 banks = flip([block("w", t, extra_w[g]) for t in range(ROW_TILES)])
             if g in extra_x:
                 banks = flip([block("x", extra_x[g], MAIN_PASSES + j) for j in range(TAIL_PASSES)])
-            if g > 0:
-                multiply_pass(g - 1)
+            if g >= LAG:
+                multiply_pass(g - LAG)
             x_units[g] = quantise(x_grouped, "x")
             for name, later in todo[0:1]:
                 split_pass(name, later)
@@ -212,7 +213,8 @@ def tile_mylayerfunc_k_kernel(tc, x, weight, out):
                 tile_units[extra_x[g]] = quantise(regroup(banks, "a", ("scalar", "scalar")), "x_tail")
 
         def multiply_tile(t, units):
-            mx_pass(t, x_units[MAIN_PASSES - 1], t, w_units[MAIN_PASSES - 1], False, False)
+            for g in range(MAIN_PASSES - LAG, MAIN_PASSES):
+                mx_pass(t, x_units[g], t, w_units[g], False, False)
             for j in range(TAIL_PASSES):
                 mx_pass(t, units, j, w_units[MAIN_PASSES + j], False, j == TAIL_PASSES - 1)
 

@@ -19,8 +19,10 @@ ROW_TILES = ROWS // P
 K_PASS = 4 * P
 PASSES = K // K_PASS
 LOAD_PASSES = 2
+SINGLE_LOADS = 4
 STAGE_BUFS = 4
 RUN = 16
+EARLY = 2
 LAG = 2
 AHEAD = 2
 UNIT = 4
@@ -44,7 +46,7 @@ def tile_mylayerfunc_k_kernel(tc, x, weight, out):
         x_split = ctx.enter_context(tc.tile_pool(name="x_split", bufs=AHEAD + 2))
         x_last = ctx.enter_context(tc.tile_pool(name="x_last", bufs=TAIL_PASSES))
         w_split = ctx.enter_context(tc.tile_pool(name="w_split", bufs=AHEAD + 4))
-        work = ctx.enter_context(tc.tile_pool(name="work", bufs=3))
+        work = ctx.enter_context(tc.tile_pool(name="work", bufs=2))
         x_mx = ctx.enter_context(tc.tile_pool(name="x_mx", bufs=LAG + 2))
         x_tail = ctx.enter_context(tc.tile_pool(name="x_tail", bufs=ROW_TILES))
         w_mx = ctx.enter_context(tc.tile_pool(name="w_mx", bufs=LAG + 2))
@@ -76,7 +78,7 @@ def tile_mylayerfunc_k_kernel(tc, x, weight, out):
         chunk_order = []
         for name, g in [item for items in needs for item in items]:
             if (name, g) not in chunk_of:
-                first, passes = (g, 1) if g < LOAD_PASSES else (g - g % LOAD_PASSES, LOAD_PASSES)
+                first, passes = (g, 1) if g < SINGLE_LOADS else (g - g % LOAD_PASSES, LOAD_PASSES)
                 chunk_order.append((name, first, passes))
                 for j in range(passes):
                     chunk_of[(name, first + j)] = first
@@ -136,7 +138,7 @@ def tile_mylayerfunc_k_kernel(tc, x, weight, out):
 
         def flip(blocks):
             banks = []
-            for half in range(2):
+            for half in range(len(blocks) // 2):
                 bank = flipped.tile([P, 2, 2, P], F32, name="bank")
                 for r in range(2):
                     for u in range(2):
@@ -144,16 +146,16 @@ def tile_mylayerfunc_k_kernel(tc, x, weight, out):
                 banks.append(bank)
             return banks
 
-        def regroup(banks, name, engines):
+        def empty_bank(bank, grouped, half):
+            dst = grouped[:, half * 1024 : (half + 1) * 1024].bitcast(F32)
+            nc.scalar.copy(
+                out=dst.rearrange("p (r m u) -> p r m u", r=2, u=2), in_=bank[:].rearrange("p r u m -> p r m u")
+            )
+
+        def regroup(banks, name):
             grouped = work.tile([P, UNIT * P * 4], BF16, name="grouped_" + name, align_bytes=64)
-            for half in range(2):
-                dst = grouped[:, half * 1024 : (half + 1) * 1024].bitcast(F32)
-                dst = dst.rearrange("p (r m u) -> p r m u", r=2, u=2)
-                src = banks[half][:].rearrange("p r u m -> p r m u")
-                if engines[half] == "vector":
-                    nc.vector.tensor_copy(out=dst, in_=src)
-                else:
-                    nc.scalar.copy(out=dst, in_=src)
+            for half, bank in enumerate(banks):
+                empty_bank(bank, grouped, half)
             return grouped
 
         def quantise(grouped, name):
@@ -161,11 +163,6 @@ def tile_mylayerfunc_k_kernel(tc, x, weight, out):
             scales = mx_pool[name].tile([P, UNIT * P], U8, name="scales_" + name, align_bytes=64)
             nc.vector.quantize_mx(out=codes[:].bitcast(FP8X4), scales=scales[:], in_=grouped[:])
             return codes, scales
-
-        def empty_round(banks, last_engine):
-            first = regroup(banks[0:2], "a", ("scalar", "scalar"))
-            second = regroup(banks[2:4], "b", ("scalar", last_engine))
-            return first, second
 
         def mx_pass(t, x_unit, j, w_unit, start, stop):
             cols = slice(j * P, (j + 1) * P)
@@ -183,8 +180,8 @@ def tile_mylayerfunc_k_kernel(tc, x, weight, out):
         w_units = {}
         tile_units = {}
 
-        def multiply_pass(g):
-            for t in range(ROW_TILES):
+        def multiply_pass(g, tiles):
+            for t in tiles:
                 mx_pass(t, x_units[g], t, w_units[g], g == 0, False)
 
         for items in needs[:AHEAD]:
@@ -192,15 +189,29 @@ def tile_mylayerfunc_k_kernel(tc, x, weight, out):
                 split_pass(name, g)
         for g in range(MAIN_PASSES):
             todo = needs[g + AHEAD] if g + AHEAD < MAIN_PASSES else []
-            banks = flip([block("x", t, g) for t in range(ROW_TILES)])
-            banks += flip([block("w", t, g) for t in range(ROW_TILES)])
-            x_grouped, w_grouped = empty_round(banks, "scalar")
             if g in extra_w:
-                banks = flip([block("w", t, extra_w[g]) for t in range(ROW_TILES)])
-            if g in extra_x:
-                banks = flip([block("x", extra_x[g], MAIN_PASSES + j) for j in range(TAIL_PASSES)])
-            if g >= LAG:
-                multiply_pass(g - LAG)
+                extra = [block("w", t, extra_w[g]) for t in range(ROW_TILES)]
+            elif g in extra_x:
+                extra = [block("x", extra_x[g], MAIN_PASSES + j) for j in range(TAIL_PASSES)]
+            else:
+                extra = []
+            half = 2 if extra else 0
+            x_banks = flip([block("x", t, g) for t in range(ROW_TILES)])
+            x_grouped = regroup(x_banks, "a")
+            extra_banks = flip(extra[0:2])
+            if extra:
+                multiply_pass(g - LAG, range(0, half))
+            w_banks = flip([block("w", t, g) for t in range(ROW_TILES)])
+            if extra:
+                e_grouped = work.tile([P, UNIT * P * 4], BF16, name="grouped_e", align_bytes=64)
+                empty_bank(extra_banks[0], e_grouped, 0)
+            w_grouped = regroup(w_banks, "b")
+            extra_banks += flip(extra[2:4])
+            if extra:
+                empty_bank(extra_banks[1], e_grouped, 1)
+            behind = 1 if g <= EARLY else LAG
+            if behind <= g and not EARLY < g < EARLY + LAG:
+                multiply_pass(g - behind, range(half, ROW_TILES))
             x_units[g] = quantise(x_grouped, "x")
             for name, later in todo[0:1]:
                 split_pass(name, later)
@@ -208,15 +219,18 @@ def tile_mylayerfunc_k_kernel(tc, x, weight, out):
             for name, later in todo[1:]:
                 split_pass(name, later)
             if g in extra_w:
-                w_units[extra_w[g]] = quantise(regroup(banks, "a", ("scalar", "scalar")), "w_last")
+                w_units[extra_w[g]] = quantise(e_grouped, "w_last")
             if g in extra_x:
-                tile_units[extra_x[g]] = quantise(regroup(banks, "a", ("scalar", "scalar")), "x_tail")
+                tile_units[extra_x[g]] = quantise(e_grouped, "x_tail")
 
         def multiply_tile(t, units):
             for g in range(MAIN_PASSES - LAG, MAIN_PASSES):
                 mx_pass(t, x_units[g], t, w_units[g], False, False)
             for j in range(TAIL_PASSES):
                 mx_pass(t, units, j, w_units[MAIN_PASSES + j], False, j == TAIL_PASSES - 1)
+
+        def engine(t):
+            return nc.gpsimd if t < ROW_TILES - 1 else nc.vector
 
         def angles(t):
             y = acc[t][:].rearrange("p (g c) -> p c g", c=NACT)
@@ -230,25 +244,22 @@ def tile_mylayerfunc_k_kernel(tc, x, weight, out):
                 out=whole[:], in0=turns[:, 1:5, :], scalar1=ROUND_MAGIC, scalar2=ROUND_MAGIC, op0=ALU.add, op1=ALU.subtract
             )
             frac = tail.tile([P, 4, GROUPS], F32, name="frac")
-            nc.vector.tensor_tensor(out=frac[:], in0=turns[:, 1:5, :], in1=whole[:], op=ALU.subtract)
+            engine(t).tensor_tensor(out=frac[:], in0=turns[:, 1:5, :], in1=whole[:], op=ALU.subtract)
             return frac, res
 
         def sines(frac, res):
             nc.scalar.activation(out=res[:, 4, :], in_=frac[:, 3, :], func=ACT.Sin, scale=TWO_PI)
             nc.scalar.activation(out=res[:, 1:4, :], in_=frac[:, 0:3, :], func=ACT.Sin, scale=TWO_PI)
 
-        def tangent(res):
+        def tangent(t, res):
             sec = tail.tile([P, GROUPS], F32, name="sec")
             nc.vector.reciprocal(out=sec[:], in_=res[:, 4, :])
-            nc.vector.tensor_mul(res[:, 3, :], res[:, 3, :], sec[:])
+            engine(t).tensor_mul(res[:, 3, :], res[:, 3, :], sec[:])
 
         def store(t, res):
             woven = tail.tile([P, GROUPS, NACT], F32, name="woven")
             by_column = res[:, 0:4, :].rearrange("p c g -> p g c")
-            if t == ROW_TILES - 1:
-                nc.vector.tensor_copy(out=woven[:], in_=by_column)
-            else:
-                nc.scalar.copy(out=woven[:], in_=by_column)
+            nc.vector.tensor_copy(out=woven[:], in_=by_column)
             nc.sync.dma_start(out=out[t * P : (t + 1) * P, :], in_=woven[:].rearrange("p g c -> p (g c)"))
 
         halfway = {}
@@ -258,6 +269,6 @@ def tile_mylayerfunc_k_kernel(tc, x, weight, out):
                 halfway[t] = angles(t)
             if 0 <= t - 1 < ROW_TILES:
                 sines(*halfway[t - 1])
-                tangent(halfway[t - 1][1])
+                tangent(t - 1, halfway[t - 1][1])
             if t - 2 >= 0:
                 store(t - 2, halfway[t - 2][1])

@@ -23,7 +23,7 @@ SINGLE_LOADS = 4
 STAGE_BUFS = 4
 RUN = 16
 EARLY = 2
-LAG = 2
+LAG = 3
 AHEAD = 2
 UNIT = 4
 TAIL_PASSES = UNIT
@@ -98,7 +98,7 @@ def tile_mylayerfunc_k_kernel(tc, x, weight, out):
                     held.pop(0)
                 held.append(first)
                 chunk_order.pop(0)
-                rows = stage.tile([P, ROW_TILES, LOAD_PASSES * K_PASS], BF16, name="rows_" + name, align_bytes=64)
+                rows = stage.tile([P, ROW_TILES, LOAD_PASSES * K_PASS], BF16, name="rows_" + name, align_bytes=256)
                 nc.sync.dma_start(
                     out=rows[:, :, 0 : passes * K_PASS],
                     in_=dram[name][:, :, first * K_PASS : (first + passes) * K_PASS],
@@ -109,7 +109,7 @@ def tile_mylayerfunc_k_kernel(tc, x, weight, out):
             first = chunk_of[(name, g)]
             gi = g - first
             pool = x_last if name == "x" and g >= MAIN_PASSES else split_pool[name]
-            halves = pool.tile([P, ROW_TILES, K_PASS], BF16, name="halves_" + name, align_bytes=64)
+            halves = pool.tile([P, ROW_TILES, K_PASS], BF16, name="halves_" + name, align_bytes=256)
             nc.vector.tensor_copy(
                 out=halves[:].rearrange("p t (h b i) -> p t h b i", h=2, i=RUN),
                 in_=staged[(name, first)][:, :, gi * K_PASS : (gi + 1) * K_PASS].rearrange(
@@ -153,14 +153,14 @@ def tile_mylayerfunc_k_kernel(tc, x, weight, out):
             )
 
         def regroup(banks, name):
-            grouped = work.tile([P, UNIT * P * 4], BF16, name="grouped_" + name, align_bytes=64)
+            grouped = work.tile([P, UNIT * P * 4], BF16, name="grouped_" + name, align_bytes=256)
             for half, bank in enumerate(banks):
                 empty_bank(bank, grouped, half)
             return grouped
 
         def quantise(grouped, name):
-            codes = mx_pool[name].tile([P, UNIT * P], U32, name="codes_" + name, align_bytes=64)
-            scales = mx_pool[name].tile([P, UNIT * P], U8, name="scales_" + name, align_bytes=64)
+            codes = mx_pool[name].tile([P, UNIT * P], U32, name="codes_" + name, align_bytes=256)
+            scales = mx_pool[name].tile([P, UNIT * P], U8, name="scales_" + name, align_bytes=256)
             nc.vector.quantize_mx(out=codes[:].bitcast(FP8X4), scales=scales[:], in_=grouped[:])
             return codes, scales
 
@@ -203,7 +203,7 @@ def tile_mylayerfunc_k_kernel(tc, x, weight, out):
                 multiply_pass(g - LAG, range(0, half))
             w_banks = flip([block("w", t, g) for t in range(ROW_TILES)])
             if extra:
-                e_grouped = work.tile([P, UNIT * P * 4], BF16, name="grouped_e", align_bytes=64)
+                e_grouped = work.tile([P, UNIT * P * 4], BF16, name="grouped_e", align_bytes=256)
                 empty_bank(extra_banks[0], e_grouped, 0)
             w_grouped = regroup(w_banks, "b")
             extra_banks += flip(extra[2:4])

@@ -22,12 +22,10 @@ LOAD_PASSES = 2
 SINGLE_LOADS = 4
 STAGE_BUFS = 4
 RUN = 16
-EARLY = 2
-LAG = 3
+DEFERRED = 24
+LAG = DEFERRED // ROW_TILES + 1
 AHEAD = 2
 UNIT = 4
-TAIL_PASSES = UNIT
-MAIN_PASSES = PASSES - TAIL_PASSES
 NACT = 4
 GROUPS = ROWS // NACT
 BANK = 512
@@ -44,13 +42,10 @@ def tile_mylayerfunc_k_kernel(tc, x, weight, out):
         const = ctx.enter_context(tc.tile_pool(name="const", bufs=1))
         stage = ctx.enter_context(tc.tile_pool(name="stage", bufs=STAGE_BUFS))
         x_split = ctx.enter_context(tc.tile_pool(name="x_split", bufs=AHEAD + 2))
-        x_last = ctx.enter_context(tc.tile_pool(name="x_last", bufs=TAIL_PASSES))
-        w_split = ctx.enter_context(tc.tile_pool(name="w_split", bufs=AHEAD + 4))
+        w_split = ctx.enter_context(tc.tile_pool(name="w_split", bufs=AHEAD + 2))
         work = ctx.enter_context(tc.tile_pool(name="work", bufs=2))
         x_mx = ctx.enter_context(tc.tile_pool(name="x_mx", bufs=LAG + 2))
-        x_tail = ctx.enter_context(tc.tile_pool(name="x_tail", bufs=ROW_TILES))
         w_mx = ctx.enter_context(tc.tile_pool(name="w_mx", bufs=LAG + 2))
-        w_last = ctx.enter_context(tc.tile_pool(name="w_last", bufs=TAIL_PASSES))
         tail = ctx.enter_context(tc.tile_pool(name="tail", bufs=3))
         flipped = ctx.enter_context(tc.psum_pool(name="flipped", bufs=4))
         sums = ctx.enter_context(tc.psum_pool(name="sums", bufs=1))
@@ -60,28 +55,17 @@ def tile_mylayerfunc_k_kernel(tc, x, weight, out):
             "x": x.rearrange("(t p) k -> p t k", p=P),
             "w": weight.rearrange("(t p) k -> p t k", p=P),
         }
-        mx_pool = {"x": x_mx, "w": w_mx, "w_last": w_last, "x_tail": x_tail}
+        mx_pool = {"x": x_mx, "w": w_mx}
         split_pool = {"x": x_split, "w": w_split}
-
-        needs = [[("x", g), ("w", g)] for g in range(MAIN_PASSES)]
-        extra_w = {}
-        extra_x = {}
-        for j in range(TAIL_PASSES):
-            g = MAIN_PASSES - 3 * TAIL_PASSES + 2 * j
-            extra_w[g] = MAIN_PASSES + j
-            needs[g].append(("w", MAIN_PASSES + j))
-            needs[g + 1].append(("x", MAIN_PASSES + j))
-        for t in range(ROW_TILES):
-            extra_x[MAIN_PASSES - ROW_TILES + t] = t
 
         chunk_of = {}
         chunk_order = []
-        for name, g in [item for items in needs for item in items]:
-            if (name, g) not in chunk_of:
+        for g in range(PASSES):
+            for name in ("x", "w"):
                 first, passes = (g, 1) if g < SINGLE_LOADS else (g - g % LOAD_PASSES, LOAD_PASSES)
-                chunk_order.append((name, first, passes))
-                for j in range(passes):
-                    chunk_of[(name, first + j)] = first
+                chunk_of[(name, g)] = first
+                if (name, first, passes) not in chunk_order:
+                    chunk_order.append((name, first, passes))
 
         staged = {}
         in_use = {"x": [], "w": []}
@@ -108,8 +92,7 @@ def tile_mylayerfunc_k_kernel(tc, x, weight, out):
         def split_pass(name, g):
             first = chunk_of[(name, g)]
             gi = g - first
-            pool = x_last if name == "x" and g >= MAIN_PASSES else split_pool[name]
-            halves = pool.tile([P, ROW_TILES, K_PASS], BF16, name="halves_" + name, align_bytes=256)
+            halves = split_pool[name].tile([P, ROW_TILES, K_PASS], BF16, name="halves_" + name, align_bytes=256)
             nc.vector.tensor_copy(
                 out=halves[:].rearrange("p t (h b i) -> p t h b i", h=2, i=RUN),
                 in_=staged[(name, first)][:, :, gi * K_PASS : (gi + 1) * K_PASS].rearrange(
@@ -178,56 +161,36 @@ def tile_mylayerfunc_k_kernel(tc, x, weight, out):
 
         x_units = {}
         w_units = {}
-        tile_units = {}
+        to_multiply = [(g, t) for g in range(PASSES) for t in range(ROW_TILES)]
 
-        def multiply_pass(g, tiles):
-            for t in tiles:
-                mx_pass(t, x_units[g], t, w_units[g], g == 0, False)
+        def multiply(passes):
+            for turn in range(passes):
+                g, t = to_multiply.pop(0)
+                mx_pass(t, x_units[g], t, w_units[g], g == 0, g == PASSES - 1)
+            return passes
 
-        for items in needs[:AHEAD]:
-            for name, g in items:
-                split_pass(name, g)
-        for g in range(MAIN_PASSES):
-            todo = needs[g + AHEAD] if g + AHEAD < MAIN_PASSES else []
-            if g in extra_w:
-                extra = [block("w", t, extra_w[g]) for t in range(ROW_TILES)]
-            elif g in extra_x:
-                extra = [block("x", extra_x[g], MAIN_PASSES + j) for j in range(TAIL_PASSES)]
-            else:
-                extra = []
-            half = 2 if extra else 0
-            x_banks = flip([block("x", t, g) for t in range(ROW_TILES)])
-            x_grouped = regroup(x_banks, "a")
-            extra_banks = flip(extra[0:2])
-            if extra:
-                multiply_pass(g - LAG, range(0, half))
-            w_banks = flip([block("w", t, g) for t in range(ROW_TILES)])
-            if extra:
-                e_grouped = work.tile([P, UNIT * P * 4], BF16, name="grouped_e", align_bytes=256)
-                empty_bank(extra_banks[0], e_grouped, 0)
-            w_grouped = regroup(w_banks, "b")
-            extra_banks += flip(extra[2:4])
-            if extra:
-                empty_bank(extra_banks[1], e_grouped, 1)
-            behind = 1 if g <= EARLY else LAG
-            if behind <= g and not EARLY < g < EARLY + LAG:
-                multiply_pass(g - behind, range(half, ROW_TILES))
+        def due(g):
+            return max(ROW_TILES * g - min(max(g - 1, 0), DEFERRED), 0)
+
+        for g in range(AHEAD):
+            split_pass("x", g)
+            split_pass("w", g)
+        multiplied = 0
+        for g in range(PASSES):
+            x_grouped = regroup(flip([block("x", t, g) for t in range(ROW_TILES)]), "a")
+            w_grouped = regroup(flip([block("w", t, g) for t in range(ROW_TILES)]), "b")
+            multiplied += multiply(due(g) - multiplied)
             x_units[g] = quantise(x_grouped, "x")
-            for name, later in todo[0:1]:
-                split_pass(name, later)
+            if g + AHEAD < PASSES:
+                split_pass("x", g + AHEAD)
             w_units[g] = quantise(w_grouped, "w")
-            for name, later in todo[1:]:
-                split_pass(name, later)
-            if g in extra_w:
-                w_units[extra_w[g]] = quantise(e_grouped, "w_last")
-            if g in extra_x:
-                tile_units[extra_x[g]] = quantise(e_grouped, "x_tail")
+            if g + AHEAD < PASSES:
+                split_pass("w", g + AHEAD)
 
-        def multiply_tile(t, units):
-            for g in range(MAIN_PASSES - LAG, MAIN_PASSES):
-                mx_pass(t, x_units[g], t, w_units[g], False, False)
-            for j in range(TAIL_PASSES):
-                mx_pass(t, units, j, w_units[MAIN_PASSES + j], False, j == TAIL_PASSES - 1)
+        def multiply_tile(t):
+            for g, u in to_multiply:
+                if u == t:
+                    mx_pass(t, x_units[g], t, w_units[g], False, g == PASSES - 1)
 
         def engine(t):
             return nc.gpsimd if t < ROW_TILES - 1 else nc.vector
@@ -265,7 +228,7 @@ def tile_mylayerfunc_k_kernel(tc, x, weight, out):
         halfway = {}
         for t in range(ROW_TILES + 2):
             if t < ROW_TILES:
-                multiply_tile(t, tile_units[t])
+                multiply_tile(t)
                 halfway[t] = angles(t)
             if 0 <= t - 1 < ROW_TILES:
                 sines(*halfway[t - 1])

@@ -22,8 +22,7 @@ LOAD_PASSES = 2
 SINGLE_LOADS = 4
 STAGE_BUFS = 4
 RUN = 16
-DEFERRED = 24
-LAG = DEFERRED // ROW_TILES + 1
+LAG = 7
 AHEAD = 2
 UNIT = 4
 NACT = 4
@@ -170,7 +169,7 @@ def tile_mylayerfunc_k_kernel(tc, x, weight, out):
             return passes
 
         def due(g):
-            return max(ROW_TILES * g - min(max(g - 1, 0), DEFERRED), 0)
+            return 10 * g // 3
 
         for g in range(AHEAD):
             split_pass("x", g)

@@ -19,9 +19,10 @@ ROW_TILES = ROWS // P
 K_PASS = 4 * P
 PASSES = K // K_PASS
 LOAD_PASSES = 2
-SINGLE_LOADS = 4
+SINGLE_LOADS = 12
 STAGE_BUFS = 4
 RUN = 16
+FIRST = 4
 LAG = 7
 AHEAD = 2
 UNIT = 4
@@ -180,9 +181,12 @@ def tile_mylayerfunc_k_kernel(tc, x, weight, out):
             w_grouped = regroup(flip([block("w", t, g) for t in range(ROW_TILES)]), "b")
             multiplied += multiply(due(g) - multiplied)
             x_units[g] = quantise(x_grouped, "x")
+            if g < FIRST:
+                w_units[g] = quantise(w_grouped, "w")
             if g + AHEAD < PASSES:
                 split_pass("x", g + AHEAD)
-            w_units[g] = quantise(w_grouped, "w")
+            if g >= FIRST:
+                w_units[g] = quantise(w_grouped, "w")
             if g + AHEAD < PASSES:
                 split_pass("w", g + AHEAD)
 

@@ -18,12 +18,15 @@ K = 16384
 ROW_TILES = ROWS // P
 K_PASS = 4 * P
 PASSES = K // K_PASS
-LOAD_PASSES = 2
-SINGLE_LOADS = 12
-STAGE_BUFS = 4
+LOAD_PASSES = 1
+SINGLE_LOADS = 32
+STAGE_BUFS = 6
 RUN = 16
 FIRST = 4
-LAG = 7
+FILL = 5
+LATE = 8
+WARM = {(0, "x"): 6, (0, "w"): 2, (1, "x"): 2, (1, "w"): 2}
+LAG = 9
 AHEAD = 2
 UNIT = 4
 NACT = 4
@@ -41,12 +44,13 @@ def tile_mylayerfunc_k_kernel(tc, x, weight, out):
     with ExitStack() as ctx:
         const = ctx.enter_context(tc.tile_pool(name="const", bufs=1))
         stage = ctx.enter_context(tc.tile_pool(name="stage", bufs=STAGE_BUFS))
-        x_split = ctx.enter_context(tc.tile_pool(name="x_split", bufs=AHEAD + 2))
-        w_split = ctx.enter_context(tc.tile_pool(name="w_split", bufs=AHEAD + 2))
-        work = ctx.enter_context(tc.tile_pool(name="work", bufs=2))
+        x_split = ctx.enter_context(tc.tile_pool(name="x_split", bufs=AHEAD + 3))
+        w_split = ctx.enter_context(tc.tile_pool(name="w_split", bufs=AHEAD + 3))
+        work = ctx.enter_context(tc.tile_pool(name="work", bufs=4))
         x_mx = ctx.enter_context(tc.tile_pool(name="x_mx", bufs=LAG + 2))
         w_mx = ctx.enter_context(tc.tile_pool(name="w_mx", bufs=LAG + 2))
-        tail = ctx.enter_context(tc.tile_pool(name="tail", bufs=3))
+        tail = ctx.enter_context(tc.tile_pool(name="tail", bufs=4))
+        weaves = ctx.enter_context(tc.tile_pool(name="weaves", bufs=4))
         flipped = ctx.enter_context(tc.psum_pool(name="flipped", bufs=4))
         sums = ctx.enter_context(tc.psum_pool(name="sums", bufs=1))
         ctx.enter_context(tc.manual_schedule())
@@ -117,7 +121,13 @@ def tile_mylayerfunc_k_kernel(tc, x, weight, out):
         warm = const.tile([P, 1], F32, name="warm")
         nc.scalar.activation(out=warm[:], in_=zero[:], func=ACT.Sin)
 
+        idle = const.tile([P, BANK], BF16, name="idle")
+        nc.vector.memset(idle[:], 0.0)
         acc = [sums.tile([P, BANK], F32, name="acc%d" % t) for t in range(ROW_TILES)]
+
+        def warm(turns):
+            for turn in range(turns):
+                nc.tensor.matmul(acc[ROW_TILES - 1][:], lhsT=idle[:, 0:P], rhs=idle[:], start=True, stop=True)
 
         def flip(blocks):
             banks = []
@@ -163,78 +173,120 @@ def tile_mylayerfunc_k_kernel(tc, x, weight, out):
         w_units = {}
         to_multiply = [(g, t) for g in range(PASSES) for t in range(ROW_TILES)]
 
-        def multiply(passes):
-            for turn in range(passes):
-                g, t = to_multiply.pop(0)
+        def multiply(items):
+            for g, t in items:
+                to_multiply.remove((g, t))
                 mx_pass(t, x_units[g], t, w_units[g], g == 0, g == PASSES - 1)
-            return passes
 
         def due(g):
             return 10 * g // 3
 
+        def turn(g):
+            count = due(g) - (ROW_TILES * PASSES - len(to_multiply))
+            new = [item for item in to_multiply if g >= LATE and item[1] == 0 and item[0] < g - 1]
+            old = [item for item in to_multiply if item not in new and item[0] < g]
+            multiply(old[0 : count - len(new)] + new)
+
         for g in range(AHEAD):
             split_pass("x", g)
             split_pass("w", g)
-        multiplied = 0
         for g in range(PASSES):
+            warm(WARM.get((g, "x"), 0))
             x_grouped = regroup(flip([block("x", t, g) for t in range(ROW_TILES)]), "a")
+            warm(WARM.get((g, "w"), 0))
             w_grouped = regroup(flip([block("w", t, g) for t in range(ROW_TILES)]), "b")
-            multiplied += multiply(due(g) - multiplied)
+            turn(g)
             x_units[g] = quantise(x_grouped, "x")
             if g < FIRST:
                 w_units[g] = quantise(w_grouped, "w")
-            if g + AHEAD < PASSES:
-                split_pass("x", g + AHEAD)
-            if g >= FIRST:
+            for later in [g + AHEAD] if g < LATE else [g + AHEAD, g + AHEAD + 1]:
+                if later < PASSES and ("x", later) not in split:
+                    split_pass("x", later)
+            if FIRST <= g < LATE:
                 w_units[g] = quantise(w_grouped, "w")
-            if g + AHEAD < PASSES:
-                split_pass("w", g + AHEAD)
+            for later in [g + AHEAD] if g < LATE else [g + AHEAD, g + AHEAD + 1]:
+                if later < PASSES and ("w", later) not in split:
+                    split_pass("w", later)
+            if g >= LATE:
+                w_units[g] = quantise(w_grouped, "w")
 
         def multiply_tile(t):
             for g, u in to_multiply:
                 if u == t:
                     mx_pass(t, x_units[g], t, w_units[g], False, g == PASSES - 1)
 
-        def engine(t):
-            return nc.gpsimd if t < ROW_TILES - 1 else nc.vector
-
-        def angles(t):
+        def turns_of(t):
             y = acc[t][:].rearrange("p (g c) -> p c g", c=NACT)
-            turns = tail.tile([P, 5, GROUPS], F32, name="turns")
             res = tail.tile([P, 5, GROUPS], F32, name="res")
+            turns = tail.tile([P, 5, GROUPS], F32, name="turns")
             nc.scalar.activation(out=turns[:, 1:5:3, :], in_=y[:, 1:4:2, :], func=ACT.Copy, bias=0.25, scale=1.0 / TWO_PI)
             nc.scalar.activation(out=turns[:, 2:4, :], in_=y[:, 2:4, :], func=ACT.Copy, scale=1.0 / TWO_PI)
             nc.scalar.copy(out=res[:, 0, :], in_=y[:, 0, :])
+            return turns, res
+
+        def whole_turns(turns):
             whole = tail.tile([P, 4, GROUPS], F32, name="whole")
             nc.vector.tensor_scalar(
                 out=whole[:], in0=turns[:, 1:5, :], scalar1=ROUND_MAGIC, scalar2=ROUND_MAGIC, op0=ALU.add, op1=ALU.subtract
             )
+            return whole
+
+        def fractions(turns, whole, sub):
             frac = tail.tile([P, 4, GROUPS], F32, name="frac")
-            engine(t).tensor_tensor(out=frac[:], in0=turns[:, 1:5, :], in1=whole[:], op=ALU.subtract)
-            return frac, res
+            sub.tensor_tensor(out=frac[:], in0=turns[:, 1:5, :], in1=whole[:], op=ALU.subtract)
+            return frac
 
-        def sines(frac, res):
-            nc.scalar.activation(out=res[:, 4, :], in_=frac[:, 3, :], func=ACT.Sin, scale=TWO_PI)
-            nc.scalar.activation(out=res[:, 1:4, :], in_=frac[:, 0:3, :], func=ACT.Sin, scale=TWO_PI)
+        def sines(frac, res, lo, hi):
+            nc.scalar.activation(out=res[:, lo:hi, :], in_=frac[:, lo - 1 : hi - 1, :], func=ACT.Sin, scale=TWO_PI)
 
-        def tangent(t, res):
+        def secant(res):
             sec = tail.tile([P, GROUPS], F32, name="sec")
             nc.vector.reciprocal(out=sec[:], in_=res[:, 4, :])
-            engine(t).tensor_mul(res[:, 3, :], res[:, 3, :], sec[:])
+            return sec
 
-        def store(t, res):
-            woven = tail.tile([P, GROUPS, NACT], F32, name="woven")
-            by_column = res[:, 0:4, :].rearrange("p c g -> p g c")
-            nc.vector.tensor_copy(out=woven[:], in_=by_column)
+        def tangent(res, sec, mul):
+            mul.tensor_mul(res[:, 3, :], res[:, 3, :], sec[:])
+
+        def store(t, res, weave):
+            woven = weaves.tile([P, GROUPS, NACT], F32, name="woven")
+            weave(out=woven[:], in_=res[:, 0:4, :].rearrange("p c g -> p g c"))
             nc.sync.dma_start(out=out[t * P : (t + 1) * P, :], in_=woven[:].rearrange("p g c -> p (g c)"))
 
-        halfway = {}
-        for t in range(ROW_TILES + 2):
-            if t < ROW_TILES:
-                multiply_tile(t)
-                halfway[t] = angles(t)
-            if 0 <= t - 1 < ROW_TILES:
-                sines(*halfway[t - 1])
-                tangent(t - 1, halfway[t - 1][1])
-            if t - 2 >= 0:
-                store(t - 2, halfway[t - 2][1])
+        multiply([item for item in to_multiply if item[1] == 1][0:FILL])
+        for t in range(ROW_TILES):
+            for g, u in to_multiply:
+                if u == t:
+                    mx_pass(t, x_units[g], t, w_units[g], False, g == PASSES - 1)
+        turns, res, whole, frac, sec = {}, {}, {}, {}, {}
+        turns[0], res[0] = turns_of(0)
+        whole[0] = whole_turns(turns[0])
+        frac[0] = fractions(turns[0], whole[0], nc.vector)
+        turns[1], res[1] = turns_of(1)
+        sines(frac[0], res[0], 4, 5)
+        sines(frac[0], res[0], 1, 4)
+        whole[1] = whole_turns(turns[1])
+        frac[1] = fractions(turns[1], whole[1], nc.gpsimd)
+        sec[0] = secant(res[0])
+        tangent(res[0], sec[0], nc.gpsimd)
+        turns[2], res[2] = turns_of(2)
+        sines(frac[1], res[1], 4, 5)
+        whole[2] = whole_turns(turns[2])
+        frac[2] = fractions(turns[2], whole[2], nc.vector)
+        sec[1] = secant(res[1])
+        sines(frac[1], res[1], 1, 4)
+        tangent(res[1], sec[1], nc.gpsimd)
+        turns[3], res[3] = turns_of(3)
+        sines(frac[2], res[2], 4, 5)
+        whole[3] = whole_turns(turns[3])
+        frac[3] = fractions(turns[3], whole[3], nc.vector)
+        sec[2] = secant(res[2])
+        sines(frac[2], res[2], 1, 4)
+        tangent(res[2], sec[2], nc.gpsimd)
+        sines(frac[3], res[3], 4, 5)
+        sines(frac[3], res[3], 1, 4)
+        sec[3] = secant(res[3])
+        store(0, res[0], nc.scalar.copy)
+        store(1, res[1], nc.scalar.copy)
+        tangent(res[3], sec[3], nc.vector)
+        store(2, res[2], nc.scalar.copy)
+        store(3, res[3], nc.vector.tensor_copy)

@@ -218,26 +218,31 @@ def tile_mylayerfunc_k_kernel(tc, x, weight, out):
         def turns_of(t):
             y = acc[t][:].rearrange("p (g c) -> p c g", c=NACT)
             res = tail.tile([P, 5, GROUPS], F32, name="res")
-            turns = tail.tile([P, 5, GROUPS], F32, name="turns")
-            nc.scalar.activation(out=turns[:, 1:5:3, :], in_=y[:, 1:4:2, :], func=ACT.Copy, bias=0.25, scale=1.0 / TWO_PI)
-            nc.scalar.activation(out=turns[:, 2:4, :], in_=y[:, 2:4, :], func=ACT.Copy, scale=1.0 / TWO_PI)
+            turns = tail.tile([P, 3, GROUPS], F32, name="turns")
+            nc.scalar.activation(out=turns[:, 2, :], in_=y[:, 3, :], func=ACT.Copy, scale=1.0 / math.pi)
+            nc.scalar.activation(out=turns[:, 0, :], in_=y[:, 1, :], func=ACT.Copy, bias=0.25, scale=1.0 / TWO_PI)
+            nc.scalar.activation(out=turns[:, 1, :], in_=y[:, 2, :], func=ACT.Copy, scale=1.0 / TWO_PI)
             nc.scalar.copy(out=res[:, 0, :], in_=y[:, 0, :])
             return turns, res
 
         def whole_turns(turns):
-            whole = tail.tile([P, 4, GROUPS], F32, name="whole")
+            whole = tail.tile([P, 3, GROUPS], F32, name="whole")
             nc.vector.tensor_scalar(
-                out=whole[:], in0=turns[:, 1:5, :], scalar1=ROUND_MAGIC, scalar2=ROUND_MAGIC, op0=ALU.add, op1=ALU.subtract
+                out=whole[:], in0=turns[:], scalar1=ROUND_MAGIC, scalar2=ROUND_MAGIC, op0=ALU.add, op1=ALU.subtract
             )
             return whole
 
         def fractions(turns, whole, sub):
-            frac = tail.tile([P, 4, GROUPS], F32, name="frac")
-            sub.tensor_tensor(out=frac[:], in0=turns[:, 1:5, :], in1=whole[:], op=ALU.subtract)
+            frac = tail.tile([P, 3, GROUPS], F32, name="frac")
+            sub.tensor_tensor(out=frac[:], in0=turns[:], in1=whole[:], op=ALU.subtract)
             return frac
 
-        def sines(frac, res, lo, hi):
-            nc.scalar.activation(out=res[:, lo:hi, :], in_=frac[:, lo - 1 : hi - 1, :], func=ACT.Sin, scale=TWO_PI)
+        def cosine(frac, res):
+            nc.scalar.activation(out=res[:, 4, :], in_=frac[:, 2, :], func=ACT.Sin, bias=math.pi / 2.0, scale=math.pi)
+
+        def sines(frac, res):
+            nc.scalar.activation(out=res[:, 3, :], in_=frac[:, 2, :], func=ACT.Sin, scale=math.pi)
+            nc.scalar.activation(out=res[:, 1:3, :], in_=frac[:, 0:2, :], func=ACT.Sin, scale=TWO_PI)
 
         def secant(res):
             sec = tail.tile([P, GROUPS], F32, name="sec")
@@ -262,28 +267,28 @@ def tile_mylayerfunc_k_kernel(tc, x, weight, out):
         whole[0] = whole_turns(turns[0])
         frac[0] = fractions(turns[0], whole[0], nc.vector)
         turns[1], res[1] = turns_of(1)
-        sines(frac[0], res[0], 4, 5)
-        sines(frac[0], res[0], 1, 4)
+        cosine(frac[0], res[0])
+        sines(frac[0], res[0])
         whole[1] = whole_turns(turns[1])
         frac[1] = fractions(turns[1], whole[1], nc.gpsimd)
         sec[0] = secant(res[0])
         tangent(res[0], sec[0], nc.gpsimd)
         turns[2], res[2] = turns_of(2)
-        sines(frac[1], res[1], 4, 5)
+        cosine(frac[1], res[1])
         whole[2] = whole_turns(turns[2])
         frac[2] = fractions(turns[2], whole[2], nc.vector)
         sec[1] = secant(res[1])
-        sines(frac[1], res[1], 1, 4)
+        sines(frac[1], res[1])
         tangent(res[1], sec[1], nc.gpsimd)
         turns[3], res[3] = turns_of(3)
-        sines(frac[2], res[2], 4, 5)
+        cosine(frac[2], res[2])
         whole[3] = whole_turns(turns[3])
         frac[3] = fractions(turns[3], whole[3], nc.vector)
         sec[2] = secant(res[2])
-        sines(frac[2], res[2], 1, 4)
+        sines(frac[2], res[2])
         tangent(res[2], sec[2], nc.gpsimd)
-        sines(frac[3], res[3], 4, 5)
-        sines(frac[3], res[3], 1, 4)
+        cosine(frac[3], res[3])
+        sines(frac[3], res[3])
         sec[3] = secant(res[3])
         store(0, res[0], nc.scalar.copy)
         store(1, res[1], nc.scalar.copy)

@@ -7,6 +7,7 @@ from concourse.masks import make_identity
 F32 = mybir.dt.float32
 BF16 = mybir.dt.bfloat16
 U32 = mybir.dt.uint32
+I32 = mybir.dt.int32
 U8 = mybir.dt.uint8
 FP8X4 = mybir.dt.float8_e4m3fn_x4
 ALU = mybir.AluOpType
@@ -262,6 +263,28 @@ def tile_mylayerfunc_k_kernel(tc, x, weight, out):
             for g, u in to_multiply:
                 if u == t:
                     mx_pass(t, x_units[g], t, w_units[g], False, g == PASSES - 1)
+        def last_angles(t):
+            y = acc[t][:].rearrange("p (g c) -> p c g", c=NACT)
+            res = tail.tile([P, 5, GROUPS], F32, name="res")
+            whole = tail.tile([P, 3, GROUPS], I32, name="whole_last")
+            frac = tail.tile([P, 3, GROUPS], F32, name="frac")
+            per_turn = {2: 1.0 / math.pi, 0: 1.0 / TWO_PI, 1: 1.0 / TWO_PI}
+            for c in (2, 0, 1):
+                nc.vector.tensor_scalar(
+                    out=whole[:, c, :], in0=y[:, c + 1, :], scalar1=per_turn[c], scalar2=0.25 if c == 0 else 0.0, op0=ALU.mult, op1=ALU.add
+                )
+            for c in (2, 0, 1):
+                nc.vector.scalar_tensor_tensor(
+                    out=frac[:, c, :], in0=y[:, c + 1, :], scalar=per_turn[c], in1=whole[:, c, :], op0=ALU.mult, op1=ALU.subtract
+                )
+            nc.scalar.copy(out=res[:, 0, :], in_=y[:, 0, :])
+            return frac, res
+
+        def last_sines(frac, res):
+            nc.scalar.activation(out=res[:, 3, :], in_=frac[:, 2, :], func=ACT.Sin, scale=math.pi)
+            nc.scalar.activation(out=res[:, 1, :], in_=frac[:, 0, :], func=ACT.Sin, bias=math.pi / 2.0, scale=TWO_PI)
+            nc.scalar.activation(out=res[:, 2, :], in_=frac[:, 1, :], func=ACT.Sin, scale=TWO_PI)
+
         turns, res, whole, frac, sec = {}, {}, {}, {}, {}
         turns[0], res[0] = turns_of(0)
         whole[0] = whole_turns(turns[0])
@@ -276,21 +299,19 @@ def tile_mylayerfunc_k_kernel(tc, x, weight, out):
         turns[2], res[2] = turns_of(2)
         cosine(frac[1], res[1])
         whole[2] = whole_turns(turns[2])
-        frac[2] = fractions(turns[2], whole[2], nc.vector)
+        frac[2] = fractions(turns[2], whole[2], nc.gpsimd)
         sec[1] = secant(res[1])
         sines(frac[1], res[1])
+        store(0, res[0], nc.scalar.copy)
         tangent(res[1], sec[1], nc.gpsimd)
-        turns[3], res[3] = turns_of(3)
+        frac[3], res[3] = last_angles(3)
         cosine(frac[2], res[2])
-        whole[3] = whole_turns(turns[3])
-        frac[3] = fractions(turns[3], whole[3], nc.vector)
+        cosine(frac[3], res[3])
+        last_sines(frac[3], res[3])
         sec[2] = secant(res[2])
         sines(frac[2], res[2])
         tangent(res[2], sec[2], nc.gpsimd)
-        cosine(frac[3], res[3])
-        sines(frac[3], res[3])
         sec[3] = secant(res[3])
-        store(0, res[0], nc.scalar.copy)
         store(1, res[1], nc.scalar.copy)
         tangent(res[3], sec[3], nc.vector)
         store(2, res[2], nc.scalar.copy)

import math
from contextlib import ExitStack

import concourse.mybir as mybir
from concourse.masks import make_identity

F32 = mybir.dt.float32
BF16 = mybir.dt.bfloat16
U32 = mybir.dt.uint32
I32 = mybir.dt.int32
U8 = mybir.dt.uint8
FP8X4 = mybir.dt.float8_e4m3fn_x4
ALU = mybir.AluOpType
ACT = mybir.ActivationFunctionType

P = 128
ROWS = 512
K = 16384
ROW_TILES = ROWS // P
K_PASS = 4 * P
PASSES = K // K_PASS
LOAD_PASSES = 1
SINGLE_LOADS = 32
STAGE_BUFS = 6
RUN = 16
FIRST = 4
FILL = 5
LATE = 8
WARM = {(0, "x"): 6, (0, "w"): 2, (1, "x"): 2, (1, "w"): 2}
LAG = 9
AHEAD = 2
UNIT = 4
NACT = 4
GROUPS = ROWS // NACT
BANK = 512

TWO_PI = 2.0 * math.pi
ROUND_MAGIC = 1.5 * 2.0**23

FLOPS = 2 * ROWS * ROWS * K


def tile_mylayerfunc_k_kernel(tc, x, weight, out):
    nc = tc.nc
    with ExitStack() as ctx:
        const = ctx.enter_context(tc.tile_pool(name="const", bufs=1))
        stage = ctx.enter_context(tc.tile_pool(name="stage", bufs=STAGE_BUFS))
        x_split = ctx.enter_context(tc.tile_pool(name="x_split", bufs=AHEAD + 3))
        w_split = ctx.enter_context(tc.tile_pool(name="w_split", bufs=AHEAD + 3))
        work = ctx.enter_context(tc.tile_pool(name="work", bufs=4))
        x_mx = ctx.enter_context(tc.tile_pool(name="x_mx", bufs=LAG + 2))
        w_mx = ctx.enter_context(tc.tile_pool(name="w_mx", bufs=LAG + 2))
        tail = ctx.enter_context(tc.tile_pool(name="tail", bufs=4))
        weaves = ctx.enter_context(tc.tile_pool(name="weaves", bufs=4))
        flipped = ctx.enter_context(tc.psum_pool(name="flipped", bufs=4))
        sums = ctx.enter_context(tc.psum_pool(name="sums", bufs=1))
        ctx.enter_context(tc.manual_schedule())

        dram = {
            "x": x.rearrange("(t p) k -> p t k", p=P),
            "w": weight.rearrange("(t p) k -> p t k", p=P),
        }
        mx_pool = {"x": x_mx, "w": w_mx}
        split_pool = {"x": x_split, "w": w_split}

        chunk_of = {}
        chunk_order = []
        for g in range(PASSES):
            for name in ("x", "w"):
                first, passes = (g, 1) if g < SINGLE_LOADS else (g - g % LOAD_PASSES, LOAD_PASSES)
                chunk_of[(name, g)] = first
                if (name, first, passes) not in chunk_order:
                    chunk_order.append((name, first, passes))

        staged = {}
        in_use = {"x": [], "w": []}
        done = set()
        split = {}

        def load_what_fits():
            while chunk_order:
                name, first, passes = chunk_order[0]
                held = in_use[name]
                if len(held) == STAGE_BUFS:
                    if (name, held[0]) not in done:
                        return
                    held.pop(0)
                held.append(first)
                chunk_order.pop(0)
                rows = stage.tile([P, ROW_TILES, LOAD_PASSES * K_PASS], BF16, name="rows_" + name, align_bytes=256)
                nc.sync.dma_start(
                    out=rows[:, :, 0 : passes * K_PASS],
                    in_=dram[name][:, :, first * K_PASS : (first + passes) * K_PASS],
                )
                staged[(name, first)] = rows

        def split_pass(name, g):
            first = chunk_of[(name, g)]
            gi = g - first
            halves = split_pool[name].tile([P, ROW_TILES, K_PASS], BF16, name="halves_" + name, align_bytes=256)
            nc.vector.tensor_copy(
                out=halves[:].rearrange("p t (h b i) -> p t h b i", h=2, i=RUN),
                in_=staged[(name, first)][:, :, gi * K_PASS : (gi + 1) * K_PASS].rearrange(
                    "p t (b h i) -> p t h b i", h=2, i=RUN
                ),
            )
            split[(name, g)] = halves
            if chunk_of.get((name, g + 1)) != first:
                done.add((name, first))
                load_what_fits()

        def block(name, t, g):
            return split[(name, g)][:, t, :].bitcast(F32)

        load_what_fits()

        ident = const.tile([P, P], F32, name="ident")
        make_identity(nc, ident[:])

        zero = const.tile([P, 1], F32, name="zero")
        nc.vector.memset(zero[:], 0.0)
        warm = const.tile([P, 1], F32, name="warm")
        nc.scalar.activation(out=warm[:], in_=zero[:], func=ACT.Sin)

        idle = const.tile([P, BANK], BF16, name="idle")
        nc.vector.memset(idle[:], 0.0)
        acc = [sums.tile([P, BANK], F32, name="acc%d" % t) for t in range(ROW_TILES)]

        def warm(turns):
            for turn in range(turns):
                nc.tensor.matmul(acc[ROW_TILES - 1][:], lhsT=idle[:, 0:P], rhs=idle[:], start=True, stop=True)

        def flip(blocks):
            banks = []
            for half in range(len(blocks) // 2):
                bank = flipped.tile([P, 2, 2, P], F32, name="bank")
                for r in range(2):
                    for u in range(2):
                        nc.tensor.transpose(bank[:, r, u, :], blocks[2 * half + r][:, u * P : (u + 1) * P], ident[:])
                banks.append(bank)
            return banks

        def empty_bank(bank, grouped, half):
            dst = grouped[:, half * 1024 : (half + 1) * 1024].bitcast(F32)
            nc.scalar.copy(
                out=dst.rearrange("p (r m u) -> p r m u", r=2, u=2), in_=bank[:].rearrange("p r u m -> p r m u")
            )

        def regroup(banks, name):
            grouped = work.tile([P, UNIT * P * 4], BF16, name="grouped_" + name, align_bytes=256)
            for half, bank in enumerate(banks):
                empty_bank(bank, grouped, half)
            return grouped

        def quantise(grouped, name):
            codes = mx_pool[name].tile([P, UNIT * P], U32, name="codes_" + name, align_bytes=256)
            scales = mx_pool[name].tile([P, UNIT * P], U8, name="scales_" + name, align_bytes=256)
            nc.vector.quantize_mx(out=codes[:].bitcast(FP8X4), scales=scales[:], in_=grouped[:])
            return codes, scales

        def mx_pass(t, x_unit, j, w_unit, start, stop):
            cols = slice(j * P, (j + 1) * P)
            nc.tensor.matmul_mx(
                out=acc[t][:],
                lhsT=x_unit[0][:, cols].bitcast(FP8X4),
                lhsT_scale=x_unit[1][:, cols],
                rhs=w_unit[0][:].bitcast(FP8X4),
                rhs_scale=w_unit[1][:],
                start=start,
                stop=stop,
            )

        x_units = {}
        w_units = {}
        to_multiply = [(g, t) for g in range(PASSES) for t in range(ROW_TILES)]

        def multiply(items):
            for g, t in items:
                to_multiply.remove((g, t))
                mx_pass(t, x_units[g], t, w_units[g], g == 0, g == PASSES - 1)

        def due(g):
            return 10 * g // 3

        def turn(g):
            count = due(g) - (ROW_TILES * PASSES - len(to_multiply))
            new = [item for item in to_multiply if g >= LATE and item[1] == 0 and item[0] < g - 1]
            old = [item for item in to_multiply if item not in new and item[0] < g]
            multiply(old[0 : count - len(new)] + new)

        for g in range(AHEAD):
            split_pass("x", g)
            split_pass("w", g)
        for g in range(PASSES):
            warm(WARM.get((g, "x"), 0))
            x_grouped = regroup(flip([block("x", t, g) for t in range(ROW_TILES)]), "a")
            warm(WARM.get((g, "w"), 0))
            w_grouped = regroup(flip([block("w", t, g) for t in range(ROW_TILES)]), "b")
            turn(g)
            x_units[g] = quantise(x_grouped, "x")
            if g < FIRST:
                w_units[g] = quantise(w_grouped, "w")
            for later in [g + AHEAD] if g < LATE else [g + AHEAD, g + AHEAD + 1]:
                if later < PASSES and ("x", later) not in split:
                    split_pass("x", later)
            if FIRST <= g < LATE:
                w_units[g] = quantise(w_grouped, "w")
            for later in [g + AHEAD] if g < LATE else [g + AHEAD, g + AHEAD + 1]:
                if later < PASSES and ("w", later) not in split:
                    split_pass("w", later)
            if g >= LATE:
                w_units[g] = quantise(w_grouped, "w")

        def multiply_tile(t):
            for g, u in to_multiply:
                if u == t:
                    mx_pass(t, x_units[g], t, w_units[g], False, g == PASSES - 1)

        def turns_of(t):
            y = acc[t][:].rearrange("p (g c) -> p c g", c=NACT)
            res = tail.tile([P, 5, GROUPS], F32, name="res")
            turns = tail.tile([P, 3, GROUPS], F32, name="turns")
            nc.scalar.activation(out=turns[:, 2, :], in_=y[:, 3, :], func=ACT.Copy, scale=1.0 / math.pi)
            nc.scalar.activation(out=turns[:, 0, :], in_=y[:, 1, :], func=ACT.Copy, bias=0.25, scale=1.0 / TWO_PI)
            nc.scalar.activation(out=turns[:, 1, :], in_=y[:, 2, :], func=ACT.Copy, scale=1.0 / TWO_PI)
            nc.scalar.copy(out=res[:, 0, :], in_=y[:, 0, :])
            return turns, res

        def whole_turns(turns):
            whole = tail.tile([P, 3, GROUPS], F32, name="whole")
            nc.vector.tensor_scalar(
                out=whole[:], in0=turns[:], scalar1=ROUND_MAGIC, scalar2=ROUND_MAGIC, op0=ALU.add, op1=ALU.subtract
            )
            return whole

        def fractions(turns, whole, sub):
            frac = tail.tile([P, 3, GROUPS], F32, name="frac")
            sub.tensor_tensor(out=frac[:], in0=turns[:], in1=whole[:], op=ALU.subtract)
            return frac

        def cosine(frac, res):
            nc.scalar.activation(out=res[:, 4, :], in_=frac[:, 2, :], func=ACT.Sin, bias=math.pi / 2.0, scale=math.pi)

        def sines(frac, res):
            nc.scalar.activation(out=res[:, 3, :], in_=frac[:, 2, :], func=ACT.Sin, scale=math.pi)
            nc.scalar.activation(out=res[:, 1:3, :], in_=frac[:, 0:2, :], func=ACT.Sin, scale=TWO_PI)

        def secant(res):
            sec = tail.tile([P, GROUPS], F32, name="sec")
            nc.vector.reciprocal(out=sec[:], in_=res[:, 4, :])
            return sec

        def tangent(res, sec, mul):
            mul.tensor_mul(res[:, 3, :], res[:, 3, :], sec[:])

        def store(t, res, weave):
            woven = weaves.tile([P, GROUPS, NACT], F32, name="woven")
            weave(out=woven[:], in_=res[:, 0:4, :].rearrange("p c g -> p g c"))
            nc.sync.dma_start(out=out[t * P : (t + 1) * P, :], in_=woven[:].rearrange("p g c -> p (g c)"))

        multiply([item for item in to_multiply if item[1] == 1][0:FILL])
        for t in range(ROW_TILES):
            for g, u in to_multiply:
                if u == t:
                    mx_pass(t, x_units[g], t, w_units[g], False, g == PASSES - 1)
        def last_angles(t):
            y = acc[t][:].rearrange("p (g c) -> p c g", c=NACT)
            res = tail.tile([P, 5, GROUPS], F32, name="res")
            whole = tail.tile([P, 3, GROUPS], I32, name="whole_last")
            frac = tail.tile([P, 3, GROUPS], F32, name="frac")
            per_turn = {2: 1.0 / math.pi, 0: 1.0 / TWO_PI, 1: 1.0 / TWO_PI}
            for c in (2, 0, 1):
                nc.vector.tensor_scalar(
                    out=whole[:, c, :], in0=y[:, c + 1, :], scalar1=per_turn[c], scalar2=0.25 if c == 0 else 0.0, op0=ALU.mult, op1=ALU.add
                )
            for c in (2, 0, 1):
                nc.vector.scalar_tensor_tensor(
                    out=frac[:, c, :], in0=y[:, c + 1, :], scalar=per_turn[c], in1=whole[:, c, :], op0=ALU.mult, op1=ALU.subtract
                )
            nc.scalar.copy(out=res[:, 0, :], in_=y[:, 0, :])
            return frac, res

        def last_sines(frac, res):
            nc.scalar.activation(out=res[:, 3, :], in_=frac[:, 2, :], func=ACT.Sin, scale=math.pi)
            nc.scalar.activation(out=res[:, 1, :], in_=frac[:, 0, :], func=ACT.Sin, bias=math.pi / 2.0, scale=TWO_PI)
            nc.scalar.activation(out=res[:, 2, :], in_=frac[:, 1, :], func=ACT.Sin, scale=TWO_PI)

        turns, res, whole, frac, sec = {}, {}, {}, {}, {}
        turns[0], res[0] = turns_of(0)
        whole[0] = whole_turns(turns[0])
        frac[0] = fractions(turns[0], whole[0], nc.vector)
        turns[1], res[1] = turns_of(1)
        cosine(frac[0], res[0])
        sines(frac[0], res[0])
        whole[1] = whole_turns(turns[1])
        frac[1] = fractions(turns[1], whole[1], nc.gpsimd)
        sec[0] = secant(res[0])
        tangent(res[0], sec[0], nc.gpsimd)
        turns[2], res[2] = turns_of(2)
        cosine(frac[1], res[1])
        whole[2] = whole_turns(turns[2])
        frac[2] = fractions(turns[2], whole[2], nc.gpsimd)
        sec[1] = secant(res[1])
        sines(frac[1], res[1])
        store(0, res[0], nc.scalar.copy)
        tangent(res[1], sec[1], nc.gpsimd)
        frac[3], res[3] = last_angles(3)
        cosine(frac[2], res[2])
        cosine(frac[3], res[3])
        last_sines(frac[3], res[3])
        sec[2] = secant(res[2])
        sines(frac[2], res[2])
        tangent(res[2], sec[2], nc.gpsimd)
        sec[3] = secant(res[3])
        store(1, res[1], nc.scalar.copy)
        tangent(res[3], sec[3], nc.vector)
        store(2, res[2], nc.scalar.copy)
        store(3, res[3], nc.vector.tensor_copy)
